import numpy as np
import ml_dtypes


def mxq(x, axis, fmt="e4m3"):
    dtype, down = {"e4m3": (ml_dtypes.float8_e4m3fn, 7), "e5m2": (ml_dtypes.float8_e5m2, 14)}[fmt]
    v = np.moveaxis(np.asarray(x, np.float32).astype(ml_dtypes.bfloat16).astype(np.float64), axis, -1)
    blocks = v.reshape(v.shape[:-1] + (-1, 32))
    amax = np.abs(blocks).max(-1, keepdims=True)
    byte = np.maximum(np.where(amax > 0, np.frexp(amax)[1] - 1 + 127, 0) - down, 1)
    scale = np.exp2(byte - 127.0)
    codes = (blocks / scale).astype(np.float32).astype(dtype).astype(np.float64)
    return np.moveaxis((codes * scale).reshape(v.shape), -1, axis)


WIDE = False


def mx_kscale(k):
    if not WIDE:
        return np.ones(k)
    levels = np.array([10, -10, 5, -5, 0])
    a = np.random.permutation(np.resize(levels, k // 512 * 4)).reshape(k // 512, 4)
    idx = np.arange(k)
    return np.exp2(a[idx // 512, idx % 128 // 32])


BF16 = ml_dtypes.bfloat16


def bf(x):
    return np.asarray(x, np.float32).astype(BF16)


def f64(x):
    return np.asarray(x).astype(np.float64)


B, S, H, I = 2, 256, 1024, 3072


def silu(v):
    return v / (1.0 + np.exp(-v))


def ternary(shape):
    return np.random.randint(-1, 2, shape).astype(np.float64)


def setup_inputs():
    s, t = mx_kscale(H), mx_kscale(I)
    x = np.random.standard_normal((B, S, H)) * s
    gate_w = ternary((I, H)) / s[None, :]
    up_w = ternary((I, H)) / s[None, :]
    down_w = ternary((H, I)) / t[None, :]
    gate_s = np.random.uniform(0.5, 2.5, I) / np.sqrt(H)
    up_s = np.random.uniform(0.5, 2.5, I) / np.sqrt(H) * t
    down_s = np.random.uniform(0.5, 2.5, H) / np.sqrt(I)
    return {"x": bf(x), "gate_w": bf(gate_w), "up_w": bf(up_w), "down_w": bf(down_w),
            "gate_s": bf(gate_s), "up_s": bf(up_s), "down_s": bf(down_s)}


def reference(x, gate_w, up_w, down_w, gate_s, up_s, down_s):
    x = f64(x)
    b, s, h = x.shape
    xq = mxq(x.reshape(b * s, h), 1, "e4m3")
    g = (xq @ mxq(f64(gate_w), 1, "e4m3").T) * f64(gate_s)
    u = (xq @ mxq(f64(up_w), 1, "e4m3").T) * f64(up_s)
    hdn = silu(g) * u
    out = (mxq(hdn, 1, "e4m3") @ mxq(f64(down_w), 1, "e4m3").T) * f64(down_s)
    return out.reshape(b, s, -1)

@@ -1,0 +1,354 @@
+from contextlib import ExitStack
+
+import concourse.mybir as mybir
+from concourse.masks import make_identity
+
+F32 = mybir.dt.float32
+BF16 = mybir.dt.bfloat16
+U32 = mybir.dt.uint32
+U8 = mybir.dt.uint8
+FP8X4 = mybir.dt.float8_e4m3fn_x4
+SILU = mybir.ActivationFunctionType.Silu
+MULT = mybir.AluOpType.mult
+
+P = 128
+TOK = 512
+H = 1024
+INNER = 3072
+UNITS = INNER // 256
+G2 = INNER // 512
+W_BUFS = 6
+FLOPS = 2 * TOK * H * 2 * INNER + 2 * TOK * INNER * H
+
+
+def tile_cudaternaryexpertmodule_kernel(
+    tc, x, gate_w, up_w, down_w, gate_s, up_s, down_s, out
+):
+    nc = tc.nc
+    xf = x.flatten_outer_dims()
+    of = out.flatten_outer_dims()
+    gate_rows = gate_w.rearrange("(a p e) h -> a p (e h)", p=P, e=2)
+    up_rows = up_w.rearrange("(a p e) h -> a p (e h)", p=P, e=2)
+    down_rows = down_w.rearrange("(b p) k -> b p k", p=P)
+
+    with ExitStack() as ctx:
+        const = ctx.enter_context(tc.tile_pool(name="const", bufs=1))
+        wpool = ctx.enter_context(tc.tile_pool(name="wpool", bufs=W_BUFS))
+        dpool = ctx.enter_context(tc.tile_pool(name="dpool", bufs=8))
+        spool = ctx.enter_context(tc.tile_pool(name="stage", bufs=3))
+        cpool = ctx.enter_context(tc.tile_pool(name="codes", bufs=3))
+        dcpool = ctx.enter_context(tc.tile_pool(name="dcodes", bufs=2))
+        epool = ctx.enter_context(tc.tile_pool(name="epi", bufs=2))
+        opool = ctx.enter_context(tc.tile_pool(name="outs", bufs=4))
+        psum = ctx.enter_context(tc.psum_pool(name="psum", bufs=1))
+        ctx.enter_context(tc.manual_schedule())
+
+        def fill(bank_no, label, srcs):
+            bk = psum.tile([P, 512], F32, name=label, tag="bank%d" % bank_no)
+            for n, src in enumerate(srcs):
+                nc.tensor.transpose(bk[:, P * n : P * (n + 1)], src, ident[:])
+            return bk
+
+        def evac(eng, dst4, bk):
+            src4 = bk[:].rearrange("p (a u m) -> p a m u", a=2, u=2, m=P)
+            if eng == "s":
+                nc.scalar.copy(out=dst4, in_=src4)
+            else:
+                nc.vector.tensor_copy(out=dst4, in_=src4)
+
+        def words512(stg, n):
+            return (
+                stg[:]
+                .bitcast(F32)[:, 512 * n : 512 * (n + 1)]
+                .rearrange("p (a m u) -> p a m u", a=2, m=P, u=2)
+            )
+
+        def quantise(stg, half, codes, scales, first_word):
+            nc.vector.quantize_mx(
+                out=codes[:, first_word : first_word + 512].bitcast(FP8X4),
+                scales=scales[:, first_word : first_word + 512],
+                in_=stg[:, 2048 * half : 2048 * (half + 1)],
+            )
+
+        warm = const.tile([P, 1], F32, name="warm")
+        warm_out = const.tile([P, 1], F32, name="warm_out")
+        nc.vector.memset(warm[:], 0.0)
+        sc_raw = const.tile([P, 256], BF16, name="sc_raw")
+        nc.vector.memset(sc_raw[:], 0.0)
+        ident = const.tile([P, P], F32, name="ident")
+        make_identity(nc, ident[:])
+        nc.scalar.dma_start(out=sc_raw[0:12, :], in_=gate_s.rearrange("(a w) -> a w", a=UNITS))
+        nc.scalar.dma_start(out=sc_raw[12:24, :], in_=up_s.rearrange("(a w) -> a w", a=UNITS))
+        nc.scalar.activation(out=warm_out[:], in_=warm[:], func=SILU)
+
+        x_sb = []
+        for tt in range(4):
+            xt = const.tile([P, H], BF16, name="x%d" % tt)
+            nc.sync.dma_start(out=xt[:], in_=xf[P * tt : P * (tt + 1), :])
+            x_sb.append(xt)
+
+        gw = {}
+        uw = {}
+
+        def load_gu(a):
+            g = wpool.tile([P, 2 * H], BF16, name="gw%d" % a, tag="gw")
+            nc.sync.dma_start(out=g[:], in_=gate_rows[a])
+            u = wpool.tile([P, 2 * H], BF16, name="uw%d" % a, tag="uw")
+            nc.sync.dma_start(out=u[:], in_=up_rows[a])
+            gw[a] = g
+            uw[a] = u
+
+        for a in range(W_BUFS):
+            load_gu(a)
+
+        dw = []
+        ds_bc = const.tile([P, H], BF16, name="ds_bc")
+
+        def load_down():
+            for b in range(8):
+                d = dpool.tile([P, INNER], BF16, name="dw%d" % b, tag="dw")
+                nc.sync.dma_start(out=d[:], in_=down_rows[b])
+                dw.append(d)
+            nc.sync.dma_start(out=ds_bc[:], in_=down_s.partition_broadcast(P))
+
+        xc = const.tile([P, 1024], U32, name="xc", align_bytes=64)
+        xs = const.tile([P, 1024], U8, name="xs", align_bytes=64)
+        hc = const.tile([P, G2 * 512], U32, name="hc", align_bytes=64)
+        hs = const.tile([P, G2 * 512], U8, name="hs", align_bytes=64)
+        sc_w = const.tile([P, 24], F32, name="sc_w")
+        sc_f = const.tile([P, 48], F32, name="sc_f")
+
+        stg_of = {}
+        wc_of = {}
+
+        def transpose_unit(a, banks):
+            bks = []
+            for j, (w, e) in enumerate(((gw[a], 0), (uw[a], 0), (gw[a], 1), (uw[a], 1))):
+                words = w[:].bitcast(F32)
+                srcs = [words[:, 512 * e + P * n : 512 * e + P * (n + 1)] for n in range(4)]
+                bks.append(fill(banks[j], "t%d_%d" % (a, j), srcs))
+            if a + W_BUFS < UNITS:
+                load_gu(a + W_BUFS)
+                if a + W_BUFS == UNITS - 1:
+                    load_down()
+            stg = spool.tile([P, 4096], BF16, name="stg%d" % a, tag="stg", align_bytes=64)
+            stg_of[a] = stg
+            return bks
+
+        def new_codes(a):
+            wc = cpool.tile([P, 1024], U32, name="wc%d" % a, tag="wc", align_bytes=64)
+            ws = cpool.tile([P, 1024], U8, name="ws%d" % a, tag="ws", align_bytes=64)
+            wc_of[a] = (wc, ws)
+
+        def quantise_unit(a, half):
+            wc, ws = wc_of[a]
+            quantise(stg_of[a], half, wc, ws, 512 * half)
+
+        def mx_unit(a):
+            wc, ws = wc_of[a]
+            bks = []
+            for j in range(4):
+                bk = psum.tile([P, 512], F32, name="m%d_%d" % (a, j), tag="bank%d" % (4 + j))
+                for g in range(2):
+                    c0 = 256 * j + P * g
+                    nc.tensor.matmul_mx(
+                        out=bk[:],
+                        lhsT=wc[:, c0 : c0 + P].bitcast(FP8X4),
+                        lhsT_scale=ws[:, c0 : c0 + P],
+                        rhs=xc[:, 512 * g : 512 * (g + 1)].bitcast(FP8X4),
+                        rhs_scale=xs[:, 512 * g : 512 * (g + 1)],
+                        start=(g == 0),
+                        stop=(g == 1),
+                    )
+                bks.append(bk)
+            return bks
+
+        sl_of = {}
+        hsb_of = {}
+        hg_of = {}
+
+        def silu(a, e, bks):
+            sl = epool.tile([P, 512], F32, name="sl%d_%d" % (a, e), tag="sl", bufs=3)
+            c = 2 * a + e
+            nc.scalar.activation(out=sl[:], in_=bks[2 * e][:], func=SILU, scale=sc_f[:, c : c + 1])
+            sl_of[e] = sl
+
+        def product(a, e, bks):
+            if a % 2 == 0 and e == 0:
+                hsb = epool.tile([P, 2048], BF16, name="hsb%d" % (a // 2), tag="hsb")
+                hsb_of[a // 2] = hsb
+            t = 2 * (a % 2) + e
+            c = 24 + 2 * a + e
+            nc.vector.scalar_tensor_tensor(
+                out=hsb_of[a // 2][:, 512 * t : 512 * (t + 1)],
+                in0=bks[2 * e + 1][:],
+                scalar=sc_f[:, c : c + 1],
+                in1=sl_of[e][:],
+                op0=MULT,
+                op1=MULT,
+            )
+
+        def regroup(g2):
+            hg = epool.tile([P, 2048], BF16, name="hg%d" % g2, tag="hg", align_bytes=64)
+            hg_of[g2] = hg
+            nc.vector.tensor_copy(
+                out=hg[:].rearrange("p (c i t) -> p c t i", c=P, i=4, t=4),
+                in_=hsb_of[g2][:].rearrange("p (t c i) -> p c t i", t=4, c=P, i=4),
+            )
+
+        def quantise_hidden(g2):
+            nc.vector.quantize_mx(
+                out=hc[:, 512 * g2 : 512 * (g2 + 1)].bitcast(FP8X4),
+                scales=hs[:, 512 * g2 : 512 * (g2 + 1)],
+                in_=hg_of[g2][:],
+            )
+
+        dstg_of = {}
+        dc_of = {}
+
+        def down_fill(q, g2, bank_no):
+            srcs = []
+            for bb in range(2):
+                words = dw[2 * q + bb][:].bitcast(F32)
+                for u in range(2):
+                    c0 = 256 * g2 + P * u
+                    srcs.append(words[:, c0 : c0 + P])
+            return fill(bank_no, "d%d_%d" % (q, g2), srcs)
+
+        def down_evac(eng, q, g2, bk):
+            if g2 % 4 == 0:
+                stg = spool.tile(
+                    [P, 4096], BF16, name="dstg%d_%d" % (q, g2 // 4), tag="stg", align_bytes=64
+                )
+                dstg_of[(q, g2 // 4)] = stg
+            evac(eng, words512(dstg_of[(q, g2 // 4)], g2 % 4), bk)
+
+        def down_quantise(q, pair):
+            if pair == 0:
+                dc = dcpool.tile([P, G2 * 256], U32, name="dc%d" % q, tag="dc", align_bytes=64)
+                dsc = dcpool.tile([P, G2 * 256], U8, name="dsc%d" % q, tag="dsc", align_bytes=64)
+                dc_of[q] = (dc, dsc)
+            dc, dsc = dc_of[q]
+            quantise(dstg_of[(q, pair // 2)], pair % 2, dc, dsc, 512 * pair)
+
+        def mx2_pass(q, tt, g2, dst):
+            dc, dsc = dc_of[q]
+            c0 = 512 * g2 + P * tt
+            nc.tensor.matmul_mx(
+                out=dst,
+                lhsT=hc[:, c0 : c0 + P].bitcast(FP8X4),
+                lhsT_scale=hs[:, c0 : c0 + P],
+                rhs=dc[:, 256 * g2 : 256 * (g2 + 1)].bitcast(FP8X4),
+                rhs_scale=dsc[:, 256 * g2 : 256 * (g2 + 1)],
+                start=(g2 == 0),
+                stop=(g2 == G2 - 1),
+            )
+
+        def final(q, tt, src):
+            o = opool.tile([P, 256], F32, name="o%d_%d" % (q, tt), tag="o")
+            nc.vector.tensor_tensor(
+                out=o[:], in0=src, in1=ds_bc[:, 256 * q : 256 * (q + 1)], op=MULT
+            )
+            nc.sync.dma_start(
+                out=of[P * tt : P * (tt + 1), 256 * q : 256 * (q + 1)], in_=o[:]
+            )
+
+        xg = spool.tile([P, 4096], BF16, name="xg", tag="stg", align_bytes=64)
+        xg4 = xg[:].bitcast(F32).rearrange("p (g w u) -> p g w u", g=2, w=TOK, u=2)
+        for tt in range(4):
+            words = x_sb[tt][:].bitcast(F32)
+            bk = fill(tt, "tx%d" % tt, [words[:, P * n : P * (n + 1)] for n in range(4)])
+            evac("v" if tt % 2 == 0 else "s", xg4[:, :, P * tt : P * (tt + 1), :], bk)
+
+        bk = fill(7, "tsc", [sc_raw[:].bitcast(F32)])
+        nc.vector.tensor_copy(out=sc_w[:], in_=bk[:, 0:24])
+        nc.vector.tensor_copy(out=sc_f[:], in_=sc_w[:].bitcast(BF16))
+        quantise(xg, 0, xc, xs, 0)
+        quantise(xg, 1, xc, xs, 512)
+
+        bks = transpose_unit(0, (4, 5, 6, 7))
+        new_codes(0)
+        evac("s", words512(stg_of[0], 0), bks[0])
+        evac("s", words512(stg_of[0], 1), bks[1])
+        quantise_unit(0, 0)
+        evac("s", words512(stg_of[0], 2), bks[2])
+        evac("v", words512(stg_of[0], 3), bks[3])
+        quantise_unit(0, 1)
+
+        bks = transpose_unit(1, (0, 1, 2, 3))
+        for j in range(4):
+            evac("s", words512(stg_of[1], j), bks[j])
+
+        early = ((0, 0), (0, 1), (0, 2), (0, 3), (0, 4), (0, 5), (1, 0), (1, 1))
+        for a in range(UNITS):
+            mbks = mx_unit(a)
+            if a + 2 < UNITS:
+                tbks = transpose_unit(a + 2, (0, 1, 2, 3))
+            else:
+                part = early[4 * (a - 10) : 4 * (a - 10) + 4]
+                tbks = [down_fill(q, g2, n) for n, (q, g2) in enumerate(part)]
+            silu(a, 0, mbks)
+            silu(a, 1, mbks)
+            for j in range(4):
+                if a + 2 < UNITS:
+                    evac("s", words512(stg_of[a + 2], j), tbks[j])
+                else:
+                    q, g2 = early[4 * (a - 10) + j]
+                    down_evac("s", q, g2, tbks[j])
+            if a + 1 < UNITS:
+                new_codes(a + 1)
+                quantise_unit(a + 1, 0)
+                quantise_unit(a + 1, 1)
+            else:
+                down_quantise(0, 0)
+                down_quantise(0, 1)
+            if a % 2 == 0 and a >= 2:
+                quantise_hidden(a // 2 - 1)
+            product(a, 0, mbks)
+            product(a, 1, mbks)
+            if a % 2 == 1:
+                regroup(a // 2)
+
+        tbks = [down_fill(1, g2, 2 + g2) for g2 in range(2, 6)]
+        for g2 in range(2, 6):
+            down_evac("s", 1, g2, tbks[g2 - 2])
+        down_quantise(0, 2)
+        quantise_hidden(G2 - 1)
+        down_quantise(1, 0)
+
+        obks = []
+        for tt in range(4):
+            ob = psum.tile([P, 512], F32, name="o0_%d" % tt, tag="bank%d" % tt)
+            obks.append(ob)
+        for g2 in range(G2):
+            for tt in range(4):
+                mx2_pass(0, tt, g2, obks[tt][:, 0:256])
+        down_quantise(1, 1)
+        down_quantise(1, 2)
+        for tt in range(4):
+            final(0, tt, obks[tt][:, 0:256])
+
+        ring = (4, 5, 6, 7, 0, 1)
+        for q in (2, 3):
+            tbks = [down_fill(q, g2, ring[g2]) for g2 in range(G2)]
+            for g2 in range(G2):
+                down_evac("s" if g2 % 2 == 0 else "v", q, g2, tbks[g2])
+                if g2 == 3:
+                    down_quantise(q, 0)
+            down_quantise(q, 1)
+            down_quantise(q, 2)
+            obks = []
+            for n in range(2):
+                ob = psum.tile([P, 512], F32, name="o%d_%d" % (q - 1, n), tag="bank%d" % (2 + n))
+                obks.append(ob)
+                for half in range(2):
+                    for g2 in range(G2):
+                        mx2_pass(q - 1, 2 * n + half, g2, ob[:, 256 * half : 256 * (half + 1)])
+            for tt in range(4):
+                final(q - 1, tt, obks[tt // 2][:, 256 * (tt % 2) : 256 * (tt % 2 + 1)])
+
+        for tt in range(4):
+            ob = psum.tile([P, 512], F32, name="o3_%d" % tt, tag="bank%d" % (4 + tt))
+            for g2 in range(G2):
+                mx2_pass(3, tt, g2, ob[:, 0:256])
+            final(3, tt, ob[:, 0:256])

@@ -43,8 +43,15 @@ def tile_cudaternaryexpertmodule_kernel(
         psum = ctx.enter_context(tc.psum_pool(name="psum", bufs=1))
         ctx.enter_context(tc.manual_schedule())
 
-        def fill(bank_no, label, srcs):
+        def bridge(bk):
+            nc.tensor.matmul(
+                out=bk[:, 0:32], lhsT=zeros[:], rhs=zeros[:, 0:32], start=True, stop=True
+            )
+
+        def fill(bank_no, label, srcs, first=False):
             bk = psum.tile([P, 512], F32, name=label, tag="bank%d" % bank_no)
+            if first:
+                bridge(bk)
             for n, src in enumerate(srcs):
                 nc.tensor.transpose(bk[:, P * n : P * (n + 1)], src, ident[:])
             return bk
@@ -75,6 +82,8 @@ def tile_cudaternaryexpertmodule_kernel(
         nc.vector.memset(warm[:], 0.0)
         sc_raw = const.tile([P, 256], BF16, name="sc_raw")
         nc.vector.memset(sc_raw[:], 0.0)
+        zeros = const.tile([P, P], BF16, name="zeros")
+        nc.vector.memset(zeros[:], 0.0)
         ident = const.tile([P, P], F32, name="ident")
         make_identity(nc, ident[:])
         nc.scalar.dma_start(out=sc_raw[0:12, :], in_=gate_s.rearrange("(a w) -> a w", a=UNITS))
@@ -121,12 +130,12 @@ def tile_cudaternaryexpertmodule_kernel(
         stg_of = {}
         wc_of = {}
 
-        def transpose_unit(a, banks):
+        def transpose_unit(a, banks, after_mx=True):
             bks = []
             for j, (w, e) in enumerate(((gw[a], 0), (uw[a], 0), (gw[a], 1), (uw[a], 1))):
                 words = w[:].bitcast(F32)
                 srcs = [words[:, 512 * e + P * n : 512 * e + P * (n + 1)] for n in range(4)]
-                bks.append(fill(banks[j], "t%d_%d" % (a, j), srcs))
+                bks.append(fill(banks[j], "t%d_%d" % (a, j), srcs, first=(after_mx and j == 0)))
             if a + W_BUFS < UNITS:
                 load_gu(a + W_BUFS)
                 if a + W_BUFS == UNITS - 1:
@@ -149,6 +158,8 @@ def tile_cudaternaryexpertmodule_kernel(
             bks = []
             for j in range(4):
                 bk = psum.tile([P, 512], F32, name="m%d_%d" % (a, j), tag="bank%d" % (4 + j))
+                if j == 0:
+                    bridge(bk)
                 for g in range(2):
                     c0 = 256 * j + P * g
                     nc.tensor.matmul_mx(
@@ -206,14 +217,14 @@ def tile_cudaternaryexpertmodule_kernel(
         dstg_of = {}
         dc_of = {}
 
-        def down_fill(q, g2, bank_no):
+        def down_fill(q, g2, bank_no, first=False):
             srcs = []
             for bb in range(2):
                 words = dw[2 * q + bb][:].bitcast(F32)
                 for u in range(2):
                     c0 = 256 * g2 + P * u
                     srcs.append(words[:, c0 : c0 + P])
-            return fill(bank_no, "d%d_%d" % (q, g2), srcs)
+            return fill(bank_no, "d%d_%d" % (q, g2), srcs, first=first)
 
         def down_evac(eng, q, g2, bk):
             if g2 % 4 == 0:
@@ -266,7 +277,7 @@ def tile_cudaternaryexpertmodule_kernel(
         quantise(xg, 0, xc, xs, 0)
         quantise(xg, 1, xc, xs, 512)
 
-        bks = transpose_unit(0, (4, 5, 6, 7))
+        bks = transpose_unit(0, (4, 5, 6, 7), after_mx=False)
         new_codes(0)
         evac("s", words512(stg_of[0], 0), bks[0])
         evac("s", words512(stg_of[0], 1), bks[1])
@@ -275,7 +286,7 @@ def tile_cudaternaryexpertmodule_kernel(
         evac("v", words512(stg_of[0], 3), bks[3])
         quantise_unit(0, 1)
 
-        bks = transpose_unit(1, (0, 1, 2, 3))
+        bks = transpose_unit(1, (0, 1, 2, 3), after_mx=False)
         for j in range(4):
             evac("s", words512(stg_of[1], j), bks[j])
 
@@ -286,7 +297,7 @@ def tile_cudaternaryexpertmodule_kernel(
                 tbks = transpose_unit(a + 2, (0, 1, 2, 3))
             else:
                 part = early[4 * (a - 10) : 4 * (a - 10) + 4]
-                tbks = [down_fill(q, g2, n) for n, (q, g2) in enumerate(part)]
+                tbks = [down_fill(q, g2, n, first=(n == 0)) for n, (q, g2) in enumerate(part)]
             silu(a, 0, mbks)
             silu(a, 1, mbks)
             for j in range(4):
@@ -320,6 +331,7 @@ def tile_cudaternaryexpertmodule_kernel(
         for tt in range(4):
             ob = psum.tile([P, 512], F32, name="o0_%d" % tt, tag="bank%d" % tt)
             obks.append(ob)
+        bridge(obks[0])
         for g2 in range(G2):
             for tt in range(4):
                 mx2_pass(0, tt, g2, obks[tt][:, 0:256])
@@ -330,7 +342,7 @@ def tile_cudaternaryexpertmodule_kernel(
 
         ring = (4, 5, 6, 7, 0, 1)
         for q in (2, 3):
-            tbks = [down_fill(q, g2, ring[g2]) for g2 in range(G2)]
+            tbks = [down_fill(q, g2, ring[g2], first=(g2 == 0)) for g2 in range(G2)]
             for g2 in range(G2):
                 down_evac("s" if g2 % 2 == 0 else "v", q, g2, tbks[g2])
                 if g2 == 3:
@@ -341,6 +353,8 @@ def tile_cudaternaryexpertmodule_kernel(
             for n in range(2):
                 ob = psum.tile([P, 512], F32, name="o%d_%d" % (q - 1, n), tag="bank%d" % (2 + n))
                 obks.append(ob)
+                if n == 0:
+                    bridge(ob)
                 for half in range(2):
                     for g2 in range(G2):
                         mx2_pass(q - 1, 2 * n + half, g2, ob[:, 256 * half : 256 * (half + 1)])

@@ -43,15 +43,17 @@ def tile_cudaternaryexpertmodule_kernel(
         psum = ctx.enter_context(tc.psum_pool(name="psum", bufs=1))
         ctx.enter_context(tc.manual_schedule())
 
-        def bridge(bk):
-            nc.tensor.matmul(
-                out=bk[:, 0:32], lhsT=zeros[:], rhs=zeros[:, 0:32], start=True, stop=True
-            )
-
-        def fill(bank_no, label, srcs, first=False):
+        def fill(bank_no, label, srcs, warm_cols=0, warm_times=1):
             bk = psum.tile([P, 512], F32, name=label, tag="bank%d" % bank_no)
-            if first:
-                bridge(bk)
+            if warm_cols > 0:
+                for n in range(warm_times):
+                    nc.tensor.matmul(
+                        out=bk[:, 0:warm_cols],
+                        lhsT=zeros[:, 0:P],
+                        rhs=zeros[:, 0:warm_cols],
+                        start=True,
+                        stop=True,
+                    )
             for n, src in enumerate(srcs):
                 nc.tensor.transpose(bk[:, P * n : P * (n + 1)], src, ident[:])
             return bk
@@ -77,13 +79,13 @@ def tile_cudaternaryexpertmodule_kernel(
                 in_=stg[:, 2048 * half : 2048 * (half + 1)],
             )
 
+        zeros = const.tile([P, 512], BF16, name="zeros")
+        nc.vector.memset(zeros[:], 0.0)
         warm = const.tile([P, 1], F32, name="warm")
         warm_out = const.tile([P, 1], F32, name="warm_out")
         nc.vector.memset(warm[:], 0.0)
         sc_raw = const.tile([P, 256], BF16, name="sc_raw")
         nc.vector.memset(sc_raw[:], 0.0)
-        zeros = const.tile([P, P], BF16, name="zeros")
-        nc.vector.memset(zeros[:], 0.0)
         ident = const.tile([P, P], F32, name="ident")
         make_identity(nc, ident[:])
         nc.scalar.dma_start(out=sc_raw[0:12, :], in_=gate_s.rearrange("(a w) -> a w", a=UNITS))
@@ -130,12 +132,12 @@ def tile_cudaternaryexpertmodule_kernel(
         stg_of = {}
         wc_of = {}
 
-        def transpose_unit(a, banks, after_mx=True):
+        def transpose_unit(a, banks, warm_cols=0):
             bks = []
             for j, (w, e) in enumerate(((gw[a], 0), (uw[a], 0), (gw[a], 1), (uw[a], 1))):
                 words = w[:].bitcast(F32)
                 srcs = [words[:, 512 * e + P * n : 512 * e + P * (n + 1)] for n in range(4)]
-                bks.append(fill(banks[j], "t%d_%d" % (a, j), srcs, first=(after_mx and j == 0)))
+                bks.append(fill(banks[j], "t%d_%d" % (a, j), srcs, warm_cols=warm_cols))
             if a + W_BUFS < UNITS:
                 load_gu(a + W_BUFS)
                 if a + W_BUFS == UNITS - 1:
@@ -158,8 +160,6 @@ def tile_cudaternaryexpertmodule_kernel(
             bks = []
             for j in range(4):
                 bk = psum.tile([P, 512], F32, name="m%d_%d" % (a, j), tag="bank%d" % (4 + j))
-                if j == 0:
-                    bridge(bk)
                 for g in range(2):
                     c0 = 256 * j + P * g
                     nc.tensor.matmul_mx(
@@ -217,14 +217,14 @@ def tile_cudaternaryexpertmodule_kernel(
         dstg_of = {}
         dc_of = {}
 
-        def down_fill(q, g2, bank_no, first=False):
+        def down_fill(q, g2, bank_no):
             srcs = []
             for bb in range(2):
                 words = dw[2 * q + bb][:].bitcast(F32)
                 for u in range(2):
                     c0 = 256 * g2 + P * u
                     srcs.append(words[:, c0 : c0 + P])
-            return fill(bank_no, "d%d_%d" % (q, g2), srcs, first=first)
+            return fill(bank_no, "d%d_%d" % (q, g2), srcs)
 
         def down_evac(eng, q, g2, bk):
             if g2 % 4 == 0:
@@ -268,7 +268,13 @@ def tile_cudaternaryexpertmodule_kernel(
         xg4 = xg[:].bitcast(F32).rearrange("p (g w u) -> p g w u", g=2, w=TOK, u=2)
         for tt in range(4):
             words = x_sb[tt][:].bitcast(F32)
-            bk = fill(tt, "tx%d" % tt, [words[:, P * n : P * (n + 1)] for n in range(4)])
+            bk = fill(
+                tt,
+                "tx%d" % tt,
+                [words[:, P * n : P * (n + 1)] for n in range(4)],
+                warm_cols=(512 if tt == 0 else 256),
+                warm_times=(4 if tt == 0 else 1),
+            )
             evac("v" if tt % 2 == 0 else "s", xg4[:, :, P * tt : P * (tt + 1), :], bk)
 
         bk = fill(7, "tsc", [sc_raw[:].bitcast(F32)])
@@ -277,7 +283,7 @@ def tile_cudaternaryexpertmodule_kernel(
         quantise(xg, 0, xc, xs, 0)
         quantise(xg, 1, xc, xs, 512)
 
-        bks = transpose_unit(0, (4, 5, 6, 7), after_mx=False)
+        bks = transpose_unit(0, (4, 5, 6, 7), warm_cols=256)
         new_codes(0)
         evac("s", words512(stg_of[0], 0), bks[0])
         evac("s", words512(stg_of[0], 1), bks[1])
@@ -286,7 +292,7 @@ def tile_cudaternaryexpertmodule_kernel(
         evac("v", words512(stg_of[0], 3), bks[3])
         quantise_unit(0, 1)
 
-        bks = transpose_unit(1, (0, 1, 2, 3), after_mx=False)
+        bks = transpose_unit(1, (0, 1, 2, 3), warm_cols=256)
         for j in range(4):
             evac("s", words512(stg_of[1], j), bks[j])
 
@@ -297,7 +303,7 @@ def tile_cudaternaryexpertmodule_kernel(
                 tbks = transpose_unit(a + 2, (0, 1, 2, 3))
             else:
                 part = early[4 * (a - 10) : 4 * (a - 10) + 4]
-                tbks = [down_fill(q, g2, n, first=(n == 0)) for n, (q, g2) in enumerate(part)]
+                tbks = [down_fill(q, g2, n) for n, (q, g2) in enumerate(part)]
             silu(a, 0, mbks)
             silu(a, 1, mbks)
             for j in range(4):
@@ -331,7 +337,6 @@ def tile_cudaternaryexpertmodule_kernel(
         for tt in range(4):
             ob = psum.tile([P, 512], F32, name="o0_%d" % tt, tag="bank%d" % tt)
             obks.append(ob)
-        bridge(obks[0])
         for g2 in range(G2):
             for tt in range(4):
                 mx2_pass(0, tt, g2, obks[tt][:, 0:256])
@@ -342,7 +347,7 @@ def tile_cudaternaryexpertmodule_kernel(
 
         ring = (4, 5, 6, 7, 0, 1)
         for q in (2, 3):
-            tbks = [down_fill(q, g2, ring[g2], first=(g2 == 0)) for g2 in range(G2)]
+            tbks = [down_fill(q, g2, ring[g2]) for g2 in range(G2)]
             for g2 in range(G2):
                 down_evac("s" if g2 % 2 == 0 else "v", q, g2, tbks[g2])
                 if g2 == 3:
@@ -353,8 +358,6 @@ def tile_cudaternaryexpertmodule_kernel(
             for n in range(2):
                 ob = psum.tile([P, 512], F32, name="o%d_%d" % (q - 1, n), tag="bank%d" % (2 + n))
                 obks.append(ob)
-                if n == 0:
-                    bridge(ob)
                 for half in range(2):
                     for g2 in range(G2):
                         mx2_pass(q - 1, 2 * n + half, g2, ob[:, 256 * half : 256 * (half + 1)])

@@ -29,6 +29,8 @@ def tile_cudaternaryexpertmodule_kernel(
     of = out.flatten_outer_dims()
     gate_rows = gate_w.rearrange("(a p e) h -> a p (e h)", p=P, e=2)
     up_rows = up_w.rearrange("(a p e) h -> a p (e h)", p=P, e=2)
+    gate_half = gate_w.rearrange("(a p e) h -> a e p h", p=P, e=2)
+    up_half = up_w.rearrange("(a p e) h -> a e p h", p=P, e=2)
     down_rows = down_w.rearrange("(b p) k -> b p k", p=P)
 
     with ExitStack() as ctx:
@@ -43,17 +45,8 @@ def tile_cudaternaryexpertmodule_kernel(
         psum = ctx.enter_context(tc.psum_pool(name="psum", bufs=1))
         ctx.enter_context(tc.manual_schedule())
 
-        def fill(bank_no, label, srcs, warm_cols=0, warm_times=1):
+        def fill(bank_no, label, srcs):
             bk = psum.tile([P, 512], F32, name=label, tag="bank%d" % bank_no)
-            if warm_cols > 0:
-                for n in range(warm_times):
-                    nc.tensor.matmul(
-                        out=bk[:, 0:warm_cols],
-                        lhsT=zeros[:, 0:P],
-                        rhs=zeros[:, 0:warm_cols],
-                        start=True,
-                        stop=True,
-                    )
             for n, src in enumerate(srcs):
                 nc.tensor.transpose(bk[:, P * n : P * (n + 1)], src, ident[:])
             return bk
@@ -79,8 +72,6 @@ def tile_cudaternaryexpertmodule_kernel(
                 in_=stg[:, 2048 * half : 2048 * (half + 1)],
             )
 
-        zeros = const.tile([P, 512], BF16, name="zeros")
-        nc.vector.memset(zeros[:], 0.0)
         warm = const.tile([P, 1], F32, name="warm")
         warm_out = const.tile([P, 1], F32, name="warm_out")
         nc.vector.memset(warm[:], 0.0)
@@ -103,9 +94,14 @@ def tile_cudaternaryexpertmodule_kernel(
 
         def load_gu(a):
             g = wpool.tile([P, 2 * H], BF16, name="gw%d" % a, tag="gw")
-            nc.sync.dma_start(out=g[:], in_=gate_rows[a])
             u = wpool.tile([P, 2 * H], BF16, name="uw%d" % a, tag="uw")
-            nc.sync.dma_start(out=u[:], in_=up_rows[a])
+            if a == 0:
+                for e in range(2):
+                    nc.sync.dma_start(out=g[:, H * e : H * (e + 1)], in_=gate_half[a, e])
+                    nc.sync.dma_start(out=u[:, H * e : H * (e + 1)], in_=up_half[a, e])
+            else:
+                nc.sync.dma_start(out=g[:], in_=gate_rows[a])
+                nc.sync.dma_start(out=u[:], in_=up_rows[a])
             gw[a] = g
             uw[a] = u
 
@@ -132,12 +128,12 @@ def tile_cudaternaryexpertmodule_kernel(
         stg_of = {}
         wc_of = {}
 
-        def transpose_unit(a, banks, warm_cols=0):
+        def transpose_unit(a, banks):
             bks = []
             for j, (w, e) in enumerate(((gw[a], 0), (uw[a], 0), (gw[a], 1), (uw[a], 1))):
                 words = w[:].bitcast(F32)
                 srcs = [words[:, 512 * e + P * n : 512 * e + P * (n + 1)] for n in range(4)]
-                bks.append(fill(banks[j], "t%d_%d" % (a, j), srcs, warm_cols=warm_cols))
+                bks.append(fill(banks[j], "t%d_%d" % (a, j), srcs))
             if a + W_BUFS < UNITS:
                 load_gu(a + W_BUFS)
                 if a + W_BUFS == UNITS - 1:
@@ -155,11 +151,11 @@ def tile_cudaternaryexpertmodule_kernel(
             wc, ws = wc_of[a]
             quantise(stg_of[a], half, wc, ws, 512 * half)
 
-        def mx_unit(a):
+        def mx_unit(a, first_bank):
             wc, ws = wc_of[a]
             bks = []
             for j in range(4):
-                bk = psum.tile([P, 512], F32, name="m%d_%d" % (a, j), tag="bank%d" % (4 + j))
+                bk = psum.tile([P, 512], F32, name="m%d_%d" % (a, j), tag="bank%d" % (first_bank + j))
                 for g in range(2):
                     c0 = 256 * j + P * g
                     nc.tensor.matmul_mx(
@@ -268,13 +264,7 @@ def tile_cudaternaryexpertmodule_kernel(
         xg4 = xg[:].bitcast(F32).rearrange("p (g w u) -> p g w u", g=2, w=TOK, u=2)
         for tt in range(4):
             words = x_sb[tt][:].bitcast(F32)
-            bk = fill(
-                tt,
-                "tx%d" % tt,
-                [words[:, P * n : P * (n + 1)] for n in range(4)],
-                warm_cols=(512 if tt == 0 else 256),
-                warm_times=(4 if tt == 0 else 1),
-            )
+            bk = fill(tt, "tx%d" % tt, [words[:, P * n : P * (n + 1)] for n in range(4)])
             evac("v" if tt % 2 == 0 else "s", xg4[:, :, P * tt : P * (tt + 1), :], bk)
 
         bk = fill(7, "tsc", [sc_raw[:].bitcast(F32)])
@@ -283,7 +273,7 @@ def tile_cudaternaryexpertmodule_kernel(
         quantise(xg, 0, xc, xs, 0)
         quantise(xg, 1, xc, xs, 512)
 
-        bks = transpose_unit(0, (4, 5, 6, 7), warm_cols=256)
+        bks = transpose_unit(0, (4, 5, 6, 7))
         new_codes(0)
         evac("s", words512(stg_of[0], 0), bks[0])
         evac("s", words512(stg_of[0], 1), bks[1])
@@ -292,13 +282,24 @@ def tile_cudaternaryexpertmodule_kernel(
         evac("v", words512(stg_of[0], 3), bks[3])
         quantise_unit(0, 1)
 
-        bks = transpose_unit(1, (0, 1, 2, 3), warm_cols=256)
+        mbks = mx_unit(0, 0)
+        bks = transpose_unit(1, (4, 5, 6, 7))
+        silu(0, 0, mbks)
+        silu(0, 1, mbks)
+        product(0, 0, mbks)
+        product(0, 1, mbks)
+        tbks = transpose_unit(2, (0, 1, 2, 3))
+        new_codes(1)
         for j in range(4):
             evac("s", words512(stg_of[1], j), bks[j])
+            if j % 2 == 1:
+                quantise_unit(1, j // 2)
+        for j in range(4):
+            evac("s", words512(stg_of[2], j), tbks[j])
 
         early = ((0, 0), (0, 1), (0, 2), (0, 3), (0, 4), (0, 5), (1, 0), (1, 1))
-        for a in range(UNITS):
-            mbks = mx_unit(a)
+        for a in range(1, UNITS):
+            mbks = mx_unit(a, 4)
             if a + 2 < UNITS:
                 tbks = transpose_unit(a + 2, (0, 1, 2, 3))
             else:

@@ -16,8 +16,11 @@ TOK = 512
 H = 1024
 INNER = 3072
 UNITS = INNER // 256
-G2 = INNER // 512
-W_BUFS = 6
+SLABS = H // P
+PASSES_2 = INNER // 512
+UNITS_IN_SBUF = 6
+BANK = 512
+STAGING = 8 * BANK
 FLOPS = 2 * TOK * H * 2 * INNER + 2 * TOK * INNER * H
 
 
@@ -29,47 +32,52 @@ def tile_cudaternaryexpertmodule_kernel(
     of = out.flatten_outer_dims()
     gate_rows = gate_w.rearrange("(a p e) h -> a p (e h)", p=P, e=2)
     up_rows = up_w.rearrange("(a p e) h -> a p (e h)", p=P, e=2)
-    gate_half = gate_w.rearrange("(a p e) h -> a e p h", p=P, e=2)
-    up_half = up_w.rearrange("(a p e) h -> a e p h", p=P, e=2)
     down_rows = down_w.rearrange("(b p) k -> b p k", p=P)
 
     with ExitStack() as ctx:
         const = ctx.enter_context(tc.tile_pool(name="const", bufs=1))
-        wpool = ctx.enter_context(tc.tile_pool(name="wpool", bufs=W_BUFS))
-        dpool = ctx.enter_context(tc.tile_pool(name="dpool", bufs=8))
-        spool = ctx.enter_context(tc.tile_pool(name="stage", bufs=3))
-        cpool = ctx.enter_context(tc.tile_pool(name="codes", bufs=3))
+        wpool = ctx.enter_context(tc.tile_pool(name="wpool", bufs=UNITS_IN_SBUF))
+        dpool = ctx.enter_context(tc.tile_pool(name="dpool", bufs=SLABS))
+        spool = ctx.enter_context(tc.tile_pool(name="stage", bufs=4))
+        cpool = ctx.enter_context(tc.tile_pool(name="codes", bufs=4))
         dcpool = ctx.enter_context(tc.tile_pool(name="dcodes", bufs=2))
         epool = ctx.enter_context(tc.tile_pool(name="epi", bufs=2))
         opool = ctx.enter_context(tc.tile_pool(name="outs", bufs=4))
         psum = ctx.enter_context(tc.psum_pool(name="psum", bufs=1))
         ctx.enter_context(tc.manual_schedule())
 
-        def fill(bank_no, label, srcs):
-            bk = psum.tile([P, 512], F32, name=label, tag="bank%d" % bank_no)
-            for n, src in enumerate(srcs):
-                nc.tensor.transpose(bk[:, P * n : P * (n + 1)], src, ident[:])
-            return bk
+        jobs = [0]
 
-        def evac(eng, dst4, bk):
-            src4 = bk[:].rearrange("p (a u m) -> p a m u", a=2, u=2, m=P)
-            if eng == "s":
-                nc.scalar.copy(out=dst4, in_=src4)
+        def next_bank(label):
+            bank = psum.tile([P, BANK], F32, name=label, tag="bank%d" % (jobs[0] % 8))
+            jobs[0] = jobs[0] + 1
+            return bank
+
+        def transpose_into_bank(label, squares):
+            bank = next_bank(label)
+            for n, square in enumerate(squares):
+                nc.tensor.transpose(bank[:, P * n : P * (n + 1)], square, ident[:])
+            return bank
+
+        def copy_pairs_out(engine, dst, bank):
+            src = bank[:].rearrange("p (i s m) -> p i m s", i=2, s=2, m=P)
+            if engine == "s":
+                nc.scalar.copy(out=dst, in_=src)
             else:
-                nc.vector.tensor_copy(out=dst4, in_=src4)
+                nc.vector.tensor_copy(out=dst, in_=src)
 
-        def words512(stg, n):
+        def room_for_bank(staging, n):
             return (
-                stg[:]
-                .bitcast(F32)[:, 512 * n : 512 * (n + 1)]
-                .rearrange("p (a m u) -> p a m u", a=2, m=P, u=2)
+                staging[:]
+                .bitcast(F32)[:, BANK * n : BANK * (n + 1)]
+                .rearrange("p (i m s) -> p i m s", i=2, m=P, s=2)
             )
 
-        def quantise(stg, half, codes, scales, first_word):
+        def quantise(staging, half, words, plane, first_word):
             nc.vector.quantize_mx(
-                out=codes[:, first_word : first_word + 512].bitcast(FP8X4),
-                scales=scales[:, first_word : first_word + 512],
-                in_=stg[:, 2048 * half : 2048 * (half + 1)],
+                out=words[:, first_word : first_word + 512].bitcast(FP8X4),
+                scales=plane[:, first_word : first_word + 512],
+                in_=staging[:, 4 * BANK * half : 4 * BANK * (half + 1)],
             )
 
         warm = const.tile([P, 1], F32, name="warm")
@@ -79,294 +87,288 @@ def tile_cudaternaryexpertmodule_kernel(
         nc.vector.memset(sc_raw[:], 0.0)
         ident = const.tile([P, P], F32, name="ident")
         make_identity(nc, ident[:])
-        nc.scalar.dma_start(out=sc_raw[0:12, :], in_=gate_s.rearrange("(a w) -> a w", a=UNITS))
-        nc.scalar.dma_start(out=sc_raw[12:24, :], in_=up_s.rearrange("(a w) -> a w", a=UNITS))
+        nc.scalar.dma_start(out=sc_raw[0:UNITS, :], in_=gate_s.rearrange("(a w) -> a w", a=UNITS))
+        nc.scalar.dma_start(
+            out=sc_raw[UNITS : 2 * UNITS, :], in_=up_s.rearrange("(a w) -> a w", a=UNITS)
+        )
         nc.scalar.activation(out=warm_out[:], in_=warm[:], func=SILU)
 
         x_sb = []
-        for tt in range(4):
-            xt = const.tile([P, H], BF16, name="x%d" % tt)
-            nc.sync.dma_start(out=xt[:], in_=xf[P * tt : P * (tt + 1), :])
-            x_sb.append(xt)
+        for tt in range(TOK // P):
+            x_tile = const.tile([P, H], BF16, name="x%d" % tt)
+            nc.sync.dma_start(out=x_tile[:], in_=xf[P * tt : P * (tt + 1), :])
+            x_sb.append(x_tile)
 
-        gw = {}
-        uw = {}
+        gate_tiles = {}
+        up_tiles = {}
 
-        def load_gu(a):
-            g = wpool.tile([P, 2 * H], BF16, name="gw%d" % a, tag="gw")
-            u = wpool.tile([P, 2 * H], BF16, name="uw%d" % a, tag="uw")
-            if a == 0:
-                for e in range(2):
-                    nc.sync.dma_start(out=g[:, H * e : H * (e + 1)], in_=gate_half[a, e])
-                    nc.sync.dma_start(out=u[:, H * e : H * (e + 1)], in_=up_half[a, e])
-            else:
-                nc.sync.dma_start(out=g[:], in_=gate_rows[a])
-                nc.sync.dma_start(out=u[:], in_=up_rows[a])
-            gw[a] = g
-            uw[a] = u
+        def load_unit(a):
+            gate_tile = wpool.tile([P, 2 * H], BF16, name="gw%d" % a, tag="gw")
+            nc.sync.dma_start(out=gate_tile[:], in_=gate_rows[a])
+            up_tile = wpool.tile([P, 2 * H], BF16, name="uw%d" % a, tag="uw")
+            nc.sync.dma_start(out=up_tile[:], in_=up_rows[a])
+            gate_tiles[a] = gate_tile
+            up_tiles[a] = up_tile
 
-        for a in range(W_BUFS):
-            load_gu(a)
+        for a in range(UNITS_IN_SBUF):
+            load_unit(a)
 
-        dw = []
-        ds_bc = const.tile([P, H], BF16, name="ds_bc")
+        slabs = []
+        down_s_all = const.tile([P, H], BF16, name="ds_bc")
 
         def load_down():
-            for b in range(8):
-                d = dpool.tile([P, INNER], BF16, name="dw%d" % b, tag="dw")
-                nc.sync.dma_start(out=d[:], in_=down_rows[b])
-                dw.append(d)
-            nc.sync.dma_start(out=ds_bc[:], in_=down_s.partition_broadcast(P))
+            for b in range(SLABS):
+                slab = dpool.tile([P, INNER], BF16, name="dw%d" % b, tag="dw")
+                nc.sync.dma_start(out=slab[:], in_=down_rows[b])
+                slabs.append(slab)
+            nc.sync.dma_start(out=down_s_all[:], in_=down_s.partition_broadcast(P))
 
-        xc = const.tile([P, 1024], U32, name="xc", align_bytes=64)
-        xs = const.tile([P, 1024], U8, name="xs", align_bytes=64)
-        hc = const.tile([P, G2 * 512], U32, name="hc", align_bytes=64)
-        hs = const.tile([P, G2 * 512], U8, name="hs", align_bytes=64)
-        sc_w = const.tile([P, 24], F32, name="sc_w")
-        sc_f = const.tile([P, 48], F32, name="sc_f")
+        x_words = const.tile([P, 2 * TOK], U32, name="xc", align_bytes=64)
+        x_plane = const.tile([P, 2 * TOK], U8, name="xs", align_bytes=64)
+        hdn_words = const.tile([P, PASSES_2 * TOK], U32, name="hc", align_bytes=64)
+        hdn_plane = const.tile([P, PASSES_2 * TOK], U8, name="hs", align_bytes=64)
+        scale_pairs = const.tile([P, 2 * UNITS], F32, name="sc_w")
+        scales_f32 = const.tile([P, 4 * UNITS], F32, name="sc_f")
 
-        stg_of = {}
-        wc_of = {}
+        staging_of = {}
+        codes_of = {}
 
-        def transpose_unit(a, banks):
-            bks = []
-            for j, (w, e) in enumerate(((gw[a], 0), (uw[a], 0), (gw[a], 1), (uw[a], 1))):
-                words = w[:].bitcast(F32)
-                srcs = [words[:, 512 * e + P * n : 512 * e + P * (n + 1)] for n in range(4)]
-                bks.append(fill(banks[j], "t%d_%d" % (a, j), srcs))
-            if a + W_BUFS < UNITS:
-                load_gu(a + W_BUFS)
-                if a + W_BUFS == UNITS - 1:
+        def transpose_unit(a):
+            filled = []
+            sources = ((gate_tiles[a], 0), (up_tiles[a], 0), (gate_tiles[a], 1), (up_tiles[a], 1))
+            for j, (w_tile, e) in enumerate(sources):
+                pairs = w_tile[:].bitcast(F32)
+                squares = [pairs[:, BANK * e + P * n : BANK * e + P * (n + 1)] for n in range(4)]
+                filled.append(transpose_into_bank("t%d_%d" % (a, j), squares))
+            if a + UNITS_IN_SBUF < UNITS:
+                load_unit(a + UNITS_IN_SBUF)
+                if a + UNITS_IN_SBUF == UNITS - 1:
                     load_down()
-            stg = spool.tile([P, 4096], BF16, name="stg%d" % a, tag="stg", align_bytes=64)
-            stg_of[a] = stg
-            return bks
+            staging = spool.tile([P, STAGING], BF16, name="stg%d" % a, tag="stg", align_bytes=64)
+            staging_of[a] = staging
+            return filled
 
         def new_codes(a):
-            wc = cpool.tile([P, 1024], U32, name="wc%d" % a, tag="wc", align_bytes=64)
-            ws = cpool.tile([P, 1024], U8, name="ws%d" % a, tag="ws", align_bytes=64)
-            wc_of[a] = (wc, ws)
+            words = cpool.tile([P, 1024], U32, name="wc%d" % a, tag="wc", align_bytes=64)
+            plane = cpool.tile([P, 1024], U8, name="ws%d" % a, tag="ws", align_bytes=64)
+            codes_of[a] = (words, plane)
 
-        def quantise_unit(a, half):
-            wc, ws = wc_of[a]
-            quantise(stg_of[a], half, wc, ws, 512 * half)
+        def quantise_unit(a, e):
+            words, plane = codes_of[a]
+            quantise(staging_of[a], e, words, plane, 512 * e)
 
-        def mx_unit(a, first_bank):
-            wc, ws = wc_of[a]
-            bks = []
+        def mx_unit(a):
+            words, plane = codes_of[a]
+            sums = []
             for j in range(4):
-                bk = psum.tile([P, 512], F32, name="m%d_%d" % (a, j), tag="bank%d" % (first_bank + j))
-                for g in range(2):
-                    c0 = 256 * j + P * g
+                bank = next_bank("m%d_%d" % (a, j))
+                for k1 in range(2):
+                    w0 = 256 * j + P * k1
                     nc.tensor.matmul_mx(
-                        out=bk[:],
-                        lhsT=wc[:, c0 : c0 + P].bitcast(FP8X4),
-                        lhsT_scale=ws[:, c0 : c0 + P],
-                        rhs=xc[:, 512 * g : 512 * (g + 1)].bitcast(FP8X4),
-                        rhs_scale=xs[:, 512 * g : 512 * (g + 1)],
-                        start=(g == 0),
-                        stop=(g == 1),
+                        out=bank[:],
+                        lhsT=words[:, w0 : w0 + P].bitcast(FP8X4),
+                        lhsT_scale=plane[:, w0 : w0 + P],
+                        rhs=x_words[:, TOK * k1 : TOK * (k1 + 1)].bitcast(FP8X4),
+                        rhs_scale=x_plane[:, TOK * k1 : TOK * (k1 + 1)],
+                        start=(k1 == 0),
+                        stop=(k1 == 1),
                     )
-                bks.append(bk)
-            return bks
+                sums.append(bank)
+            return sums
 
-        sl_of = {}
-        hsb_of = {}
-        hg_of = {}
+        silu_of = {}
+        four_planes_of = {}
+        grouped_of = {}
 
-        def silu(a, e, bks):
-            sl = epool.tile([P, 512], F32, name="sl%d_%d" % (a, e), tag="sl", bufs=3)
-            c = 2 * a + e
-            nc.scalar.activation(out=sl[:], in_=bks[2 * e][:], func=SILU, scale=sc_f[:, c : c + 1])
-            sl_of[e] = sl
+        def silu(a, e, sums):
+            silu_tile = epool.tile([P, TOK], F32, name="sl%d_%d" % (a, e), tag="sl", bufs=4)
+            col = 2 * a + e
+            nc.scalar.activation(
+                out=silu_tile[:], in_=sums[2 * e][:], func=SILU, scale=scales_f32[:, col : col + 1]
+            )
+            silu_of[(a, e)] = silu_tile
 
-        def product(a, e, bks):
+        def product(a, e, sums):
             if a % 2 == 0 and e == 0:
-                hsb = epool.tile([P, 2048], BF16, name="hsb%d" % (a // 2), tag="hsb")
-                hsb_of[a // 2] = hsb
+                four = epool.tile([P, 4 * TOK], BF16, name="hsb%d" % (a // 2), tag="hsb")
+                four_planes_of[a // 2] = four
             t = 2 * (a % 2) + e
-            c = 24 + 2 * a + e
+            col = 2 * UNITS + 2 * a + e
             nc.vector.scalar_tensor_tensor(
-                out=hsb_of[a // 2][:, 512 * t : 512 * (t + 1)],
-                in0=bks[2 * e + 1][:],
-                scalar=sc_f[:, c : c + 1],
-                in1=sl_of[e][:],
+                out=four_planes_of[a // 2][:, TOK * t : TOK * (t + 1)],
+                in0=sums[2 * e + 1][:],
+                scalar=scales_f32[:, col : col + 1],
+                in1=silu_of[(a, e)][:],
                 op0=MULT,
                 op1=MULT,
             )
 
-        def regroup(g2):
-            hg = epool.tile([P, 2048], BF16, name="hg%d" % g2, tag="hg", align_bytes=64)
-            hg_of[g2] = hg
+        def regroup(k2):
+            grouped = epool.tile([P, 4 * TOK], BF16, name="hg%d" % k2, tag="hg", align_bytes=64)
+            grouped_of[k2] = grouped
             nc.vector.tensor_copy(
-                out=hg[:].rearrange("p (c i t) -> p c t i", c=P, i=4, t=4),
-                in_=hsb_of[g2][:].rearrange("p (t c i) -> p c t i", t=4, c=P, i=4),
+                out=grouped[:].rearrange("p (c i t) -> p c t i", c=P, i=4, t=4),
+                in_=four_planes_of[k2][:].rearrange("p (t c i) -> p c t i", t=4, c=P, i=4),
             )
 
-        def quantise_hidden(g2):
+        def quantise_hdn(k2):
             nc.vector.quantize_mx(
-                out=hc[:, 512 * g2 : 512 * (g2 + 1)].bitcast(FP8X4),
-                scales=hs[:, 512 * g2 : 512 * (g2 + 1)],
-                in_=hg_of[g2][:],
+                out=hdn_words[:, TOK * k2 : TOK * (k2 + 1)].bitcast(FP8X4),
+                scales=hdn_plane[:, TOK * k2 : TOK * (k2 + 1)],
+                in_=grouped_of[k2][:],
             )
 
-        dstg_of = {}
-        dc_of = {}
+        down_staging_of = {}
+        down_codes_of = {}
 
-        def down_fill(q, g2, bank_no):
-            srcs = []
-            for bb in range(2):
-                words = dw[2 * q + bb][:].bitcast(F32)
-                for u in range(2):
-                    c0 = 256 * g2 + P * u
-                    srcs.append(words[:, c0 : c0 + P])
-            return fill(bank_no, "d%d_%d" % (q, g2), srcs)
+        def transpose_down(q, k2):
+            squares = []
+            for b in range(2):
+                pairs = slabs[2 * q + b][:].bitcast(F32)
+                for s in range(2):
+                    first = 256 * k2 + P * s
+                    squares.append(pairs[:, first : first + P])
+            return transpose_into_bank("d%d_%d" % (q, k2), squares)
 
-        def down_evac(eng, q, g2, bk):
-            if g2 % 4 == 0:
-                stg = spool.tile(
-                    [P, 4096], BF16, name="dstg%d_%d" % (q, g2 // 4), tag="stg", align_bytes=64
+        def copy_down_out(engine, q, k2, bank):
+            if k2 % 4 == 0:
+                staging = spool.tile(
+                    [P, STAGING], BF16, name="dstg%d_%d" % (q, k2 // 4), tag="stg", align_bytes=64
                 )
-                dstg_of[(q, g2 // 4)] = stg
-            evac(eng, words512(dstg_of[(q, g2 // 4)], g2 % 4), bk)
+                down_staging_of[(q, k2 // 4)] = staging
+            copy_pairs_out(engine, room_for_bank(down_staging_of[(q, k2 // 4)], k2 % 4), bank)
 
-        def down_quantise(q, pair):
-            if pair == 0:
-                dc = dcpool.tile([P, G2 * 256], U32, name="dc%d" % q, tag="dc", align_bytes=64)
-                dsc = dcpool.tile([P, G2 * 256], U8, name="dsc%d" % q, tag="dsc", align_bytes=64)
-                dc_of[q] = (dc, dsc)
-            dc, dsc = dc_of[q]
-            quantise(dstg_of[(q, pair // 2)], pair % 2, dc, dsc, 512 * pair)
+        def quantise_down(q, n):
+            if n == 0:
+                words = dcpool.tile([P, PASSES_2 * 256], U32, name="dc%d" % q, tag="dc", align_bytes=64)
+                plane = dcpool.tile([P, PASSES_2 * 256], U8, name="dsc%d" % q, tag="dsc", align_bytes=64)
+                down_codes_of[q] = (words, plane)
+            words, plane = down_codes_of[q]
+            quantise(down_staging_of[(q, n // 2)], n % 2, words, plane, 512 * n)
 
-        def mx2_pass(q, tt, g2, dst):
-            dc, dsc = dc_of[q]
-            c0 = 512 * g2 + P * tt
+        def mx2_pass(q, tt, k2, dst):
+            words, plane = down_codes_of[q]
+            w0 = TOK * k2 + P * tt
             nc.tensor.matmul_mx(
                 out=dst,
-                lhsT=hc[:, c0 : c0 + P].bitcast(FP8X4),
-                lhsT_scale=hs[:, c0 : c0 + P],
-                rhs=dc[:, 256 * g2 : 256 * (g2 + 1)].bitcast(FP8X4),
-                rhs_scale=dsc[:, 256 * g2 : 256 * (g2 + 1)],
-                start=(g2 == 0),
-                stop=(g2 == G2 - 1),
+                lhsT=hdn_words[:, w0 : w0 + P].bitcast(FP8X4),
+                lhsT_scale=hdn_plane[:, w0 : w0 + P],
+                rhs=words[:, 256 * k2 : 256 * (k2 + 1)].bitcast(FP8X4),
+                rhs_scale=plane[:, 256 * k2 : 256 * (k2 + 1)],
+                start=(k2 == 0),
+                stop=(k2 == PASSES_2 - 1),
             )
 
-        def final(q, tt, src):
-            o = opool.tile([P, 256], F32, name="o%d_%d" % (q, tt), tag="o")
+        def scale_and_store(q, tt, sums):
+            out_tile = opool.tile([P, 256], F32, name="o%d_%d" % (q, tt), tag="o")
             nc.vector.tensor_tensor(
-                out=o[:], in0=src, in1=ds_bc[:, 256 * q : 256 * (q + 1)], op=MULT
+                out=out_tile[:], in0=sums, in1=down_s_all[:, 256 * q : 256 * (q + 1)], op=MULT
             )
             nc.sync.dma_start(
-                out=of[P * tt : P * (tt + 1), 256 * q : 256 * (q + 1)], in_=o[:]
+                out=of[P * tt : P * (tt + 1), 256 * q : 256 * (q + 1)], in_=out_tile[:]
             )
 
-        xg = spool.tile([P, 4096], BF16, name="xg", tag="stg", align_bytes=64)
-        xg4 = xg[:].bitcast(F32).rearrange("p (g w u) -> p g w u", g=2, w=TOK, u=2)
-        for tt in range(4):
-            words = x_sb[tt][:].bitcast(F32)
-            bk = fill(tt, "tx%d" % tt, [words[:, P * n : P * (n + 1)] for n in range(4)])
-            evac("v" if tt % 2 == 0 else "s", xg4[:, :, P * tt : P * (tt + 1), :], bk)
+        x_staging = spool.tile([P, STAGING], BF16, name="xg", tag="stg", align_bytes=64)
+        x_rooms = x_staging[:].bitcast(F32).rearrange("p (i m s) -> p i m s", i=2, m=TOK, s=2)
+        for tt in range(TOK // P):
+            pairs = x_sb[tt][:].bitcast(F32)
+            bank = transpose_into_bank("tx%d" % tt, [pairs[:, P * n : P * (n + 1)] for n in range(4)])
+            copy_pairs_out("v" if tt % 2 == 0 else "s", x_rooms[:, :, P * tt : P * (tt + 1), :], bank)
 
-        bk = fill(7, "tsc", [sc_raw[:].bitcast(F32)])
-        nc.vector.tensor_copy(out=sc_w[:], in_=bk[:, 0:24])
-        nc.vector.tensor_copy(out=sc_f[:], in_=sc_w[:].bitcast(BF16))
-        quantise(xg, 0, xc, xs, 0)
-        quantise(xg, 1, xc, xs, 512)
+        bank = transpose_into_bank("tsc", [sc_raw[:].bitcast(F32)])
+        nc.vector.tensor_copy(out=scale_pairs[:], in_=bank[:, 0 : 2 * UNITS])
+        nc.vector.tensor_copy(out=scales_f32[:], in_=scale_pairs[:].bitcast(BF16))
+        quantise(x_staging, 0, x_words, x_plane, 0)
+        quantise(x_staging, 1, x_words, x_plane, 512)
 
-        bks = transpose_unit(0, (4, 5, 6, 7))
+        filled = transpose_unit(0)
         new_codes(0)
-        evac("s", words512(stg_of[0], 0), bks[0])
-        evac("s", words512(stg_of[0], 1), bks[1])
+        copy_pairs_out("s", room_for_bank(staging_of[0], 0), filled[0])
+        copy_pairs_out("s", room_for_bank(staging_of[0], 1), filled[1])
         quantise_unit(0, 0)
-        evac("s", words512(stg_of[0], 2), bks[2])
-        evac("v", words512(stg_of[0], 3), bks[3])
+        copy_pairs_out("s", room_for_bank(staging_of[0], 2), filled[2])
+        copy_pairs_out("v", room_for_bank(staging_of[0], 3), filled[3])
         quantise_unit(0, 1)
 
-        mbks = mx_unit(0, 0)
-        bks = transpose_unit(1, (4, 5, 6, 7))
-        silu(0, 0, mbks)
-        silu(0, 1, mbks)
-        product(0, 0, mbks)
-        product(0, 1, mbks)
-        tbks = transpose_unit(2, (0, 1, 2, 3))
-        new_codes(1)
-        for j in range(4):
-            evac("s", words512(stg_of[1], j), bks[j])
-            if j % 2 == 1:
-                quantise_unit(1, j // 2)
-        for j in range(4):
-            evac("s", words512(stg_of[2], j), tbks[j])
-
-        early = ((0, 0), (0, 1), (0, 2), (0, 3), (0, 4), (0, 5), (1, 0), (1, 1))
-        for a in range(1, UNITS):
-            mbks = mx_unit(a, 4)
-            if a + 2 < UNITS:
-                tbks = transpose_unit(a + 2, (0, 1, 2, 3))
-            else:
-                part = early[4 * (a - 10) : 4 * (a - 10) + 4]
-                tbks = [down_fill(q, g2, n) for n, (q, g2) in enumerate(part)]
-            silu(a, 0, mbks)
-            silu(a, 1, mbks)
+        def copy_and_quantise_unit(a, filled_banks, hdn_pass):
+            new_codes(a)
             for j in range(4):
-                if a + 2 < UNITS:
-                    evac("s", words512(stg_of[a + 2], j), tbks[j])
-                else:
-                    q, g2 = early[4 * (a - 10) + j]
-                    down_evac("s", q, g2, tbks[j])
-            if a + 1 < UNITS:
-                new_codes(a + 1)
-                quantise_unit(a + 1, 0)
-                quantise_unit(a + 1, 1)
-            else:
-                down_quantise(0, 0)
-                down_quantise(0, 1)
-            if a % 2 == 0 and a >= 2:
-                quantise_hidden(a // 2 - 1)
-            product(a, 0, mbks)
-            product(a, 1, mbks)
-            if a % 2 == 1:
-                regroup(a // 2)
+                copy_pairs_out("s", room_for_bank(staging_of[a], j), filled_banks[j])
+                if j % 2 == 1:
+                    quantise_unit(a, j // 2)
+                    if j == 1 and hdn_pass >= 0:
+                        quantise_hdn(hdn_pass)
 
-        tbks = [down_fill(1, g2, 2 + g2) for g2 in range(2, 6)]
-        for g2 in range(2, 6):
-            down_evac("s", 1, g2, tbks[g2 - 2])
-        down_quantise(0, 2)
-        quantise_hidden(G2 - 1)
-        down_quantise(1, 0)
+        def finish_units(units, sums_of):
+            for a in units:
+                silu(a, 0, sums_of[a])
+                silu(a, 1, sums_of[a])
+            for a in units:
+                product(a, 0, sums_of[a])
+                product(a, 1, sums_of[a])
 
-        obks = []
-        for tt in range(4):
-            ob = psum.tile([P, 512], F32, name="o0_%d" % tt, tag="bank%d" % tt)
-            obks.append(ob)
-        for g2 in range(G2):
+        filled = transpose_unit(1)
+        copy_and_quantise_unit(1, filled, -1)
+        finish_units((0,), {0: mx_unit(0)})
+
+        for k in range(UNITS // 2 - 1):
+            first = 2 * k + 2
+            filled_first = transpose_unit(first)
+            filled_second = transpose_unit(first + 1)
+            copy_and_quantise_unit(first, filled_first, k - 1)
+            copy_and_quantise_unit(first + 1, filled_second, -1)
+            sums_of = {}
+            sums_of[first - 1] = mx_unit(first - 1)
+            sums_of[first] = mx_unit(first)
+            finish_units((first - 1, first), sums_of)
+            regroup(k)
+
+        first_down_banks = ((0, 0), (0, 1), (0, 2), (0, 3), (0, 4), (0, 5), (1, 0), (1, 1))
+        filled = [transpose_down(q, k2) for q, k2 in first_down_banks]
+        for n, (q, k2) in enumerate(first_down_banks):
+            copy_down_out("s", q, k2, filled[n])
+            if n % 2 == 1:
+                quantise_down(q, k2 // 2)
+                if n == 1:
+                    quantise_hdn(PASSES_2 - 2)
+        finish_units((UNITS - 1,), {UNITS - 1: mx_unit(UNITS - 1)})
+        regroup(PASSES_2 - 1)
+
+        filled = [transpose_down(1, k2) for k2 in range(2, PASSES_2)]
+        for k2 in range(2, PASSES_2):
+            copy_down_out("s", 1, k2, filled[k2 - 2])
+            if k2 == 3:
+                quantise_down(1, 1)
+                quantise_hdn(PASSES_2 - 1)
+        quantise_down(1, 2)
+
+        out_banks = [next_bank("o0_%d" % tt) for tt in range(4)]
+        for k2 in range(PASSES_2):
             for tt in range(4):
-                mx2_pass(0, tt, g2, obks[tt][:, 0:256])
-        down_quantise(1, 1)
-        down_quantise(1, 2)
+                mx2_pass(0, tt, k2, out_banks[tt][:, 0:256])
         for tt in range(4):
-            final(0, tt, obks[tt][:, 0:256])
+            scale_and_store(0, tt, out_banks[tt][:, 0:256])
 
-        ring = (4, 5, 6, 7, 0, 1)
         for q in (2, 3):
-            tbks = [down_fill(q, g2, ring[g2]) for g2 in range(G2)]
-            for g2 in range(G2):
-                down_evac("s" if g2 % 2 == 0 else "v", q, g2, tbks[g2])
-                if g2 == 3:
-                    down_quantise(q, 0)
-            down_quantise(q, 1)
-            down_quantise(q, 2)
-            obks = []
+            filled = [transpose_down(q, k2) for k2 in range(PASSES_2)]
+            for k2 in range(PASSES_2):
+                copy_down_out("s" if k2 % 2 == 0 else "v", q, k2, filled[k2])
+                if k2 == 3:
+                    quantise_down(q, 0)
+            quantise_down(q, 1)
+            quantise_down(q, 2)
+            out_banks = []
             for n in range(2):
-                ob = psum.tile([P, 512], F32, name="o%d_%d" % (q - 1, n), tag="bank%d" % (2 + n))
-                obks.append(ob)
-                for half in range(2):
-                    for g2 in range(G2):
-                        mx2_pass(q - 1, 2 * n + half, g2, ob[:, 256 * half : 256 * (half + 1)])
+                out_bank = next_bank("o%d_%d" % (q - 1, n))
+                out_banks.append(out_bank)
+                for side in range(2):
+                    for k2 in range(PASSES_2):
+                        mx2_pass(q - 1, 2 * n + side, k2, out_bank[:, 256 * side : 256 * (side + 1)])
             for tt in range(4):
-                final(q - 1, tt, obks[tt // 2][:, 256 * (tt % 2) : 256 * (tt % 2 + 1)])
+                scale_and_store(q - 1, tt, out_banks[tt // 2][:, 256 * (tt % 2) : 256 * (tt % 2 + 1)])
 
         for tt in range(4):
-            ob = psum.tile([P, 512], F32, name="o3_%d" % tt, tag="bank%d" % (4 + tt))
-            for g2 in range(G2):
-                mx2_pass(3, tt, g2, ob[:, 0:256])
-            final(3, tt, ob[:, 0:256])
+            out_bank = next_bank("o3_%d" % tt)
+            for k2 in range(PASSES_2):
+                mx2_pass(3, tt, k2, out_bank[:, 0:256])
+            scale_and_store(3, tt, out_bank[:, 0:256])

from contextlib import ExitStack

import concourse.mybir as mybir
from concourse.masks import make_identity

F32 = mybir.dt.float32
BF16 = mybir.dt.bfloat16
U32 = mybir.dt.uint32
U8 = mybir.dt.uint8
FP8X4 = mybir.dt.float8_e4m3fn_x4
SILU = mybir.ActivationFunctionType.Silu
MULT = mybir.AluOpType.mult

P = 128
TOK = 512
H = 1024
INNER = 3072
UNITS = INNER // 256
SLABS = H // P
PASSES_2 = INNER // 512
UNITS_IN_SBUF = 6
BANK = 512
STAGING = 8 * BANK
FLOPS = 2 * TOK * H * 2 * INNER + 2 * TOK * INNER * H


def tile_cudaternaryexpertmodule_kernel(
    tc, x, gate_w, up_w, down_w, gate_s, up_s, down_s, out
):
    nc = tc.nc
    xf = x.flatten_outer_dims()
    of = out.flatten_outer_dims()
    gate_rows = gate_w.rearrange("(a p e) h -> a p (e h)", p=P, e=2)
    up_rows = up_w.rearrange("(a p e) h -> a p (e h)", p=P, e=2)
    down_rows = down_w.rearrange("(b p) k -> b p k", p=P)

    with ExitStack() as ctx:
        const = ctx.enter_context(tc.tile_pool(name="const", bufs=1))
        wpool = ctx.enter_context(tc.tile_pool(name="wpool", bufs=UNITS_IN_SBUF))
        dpool = ctx.enter_context(tc.tile_pool(name="dpool", bufs=SLABS))
        spool = ctx.enter_context(tc.tile_pool(name="stage", bufs=4))
        cpool = ctx.enter_context(tc.tile_pool(name="codes", bufs=4))
        dcpool = ctx.enter_context(tc.tile_pool(name="dcodes", bufs=2))
        epool = ctx.enter_context(tc.tile_pool(name="epi", bufs=2))
        opool = ctx.enter_context(tc.tile_pool(name="outs", bufs=4))
        psum = ctx.enter_context(tc.psum_pool(name="psum", bufs=1))
        ctx.enter_context(tc.manual_schedule())

        jobs = [0]

        def next_bank(label):
            bank = psum.tile([P, BANK], F32, name=label, tag="bank%d" % (jobs[0] % 8))
            jobs[0] = jobs[0] + 1
            return bank

        def transpose_into_bank(label, squares):
            bank = next_bank(label)
            for n, square in enumerate(squares):
                nc.tensor.transpose(bank[:, P * n : P * (n + 1)], square, ident[:])
            return bank

        def copy_pairs_out(engine, dst, bank):
            src = bank[:].rearrange("p (i s m) -> p i m s", i=2, s=2, m=P)
            if engine == "s":
                nc.scalar.copy(out=dst, in_=src)
            else:
                nc.vector.tensor_copy(out=dst, in_=src)

        def room_for_bank(staging, n):
            return (
                staging[:]
                .bitcast(F32)[:, BANK * n : BANK * (n + 1)]
                .rearrange("p (i m s) -> p i m s", i=2, m=P, s=2)
            )

        def quantise(staging, half, words, plane, first_word):
            nc.vector.quantize_mx(
                out=words[:, first_word : first_word + 512].bitcast(FP8X4),
                scales=plane[:, first_word : first_word + 512],
                in_=staging[:, 4 * BANK * half : 4 * BANK * (half + 1)],
            )

        warm = const.tile([P, 1], F32, name="warm")
        warm_out = const.tile([P, 1], F32, name="warm_out")
        nc.vector.memset(warm[:], 0.0)
        sc_raw = const.tile([P, 256], BF16, name="sc_raw")
        nc.vector.memset(sc_raw[:], 0.0)
        ident = const.tile([P, P], F32, name="ident")
        make_identity(nc, ident[:])
        nc.scalar.dma_start(out=sc_raw[0:UNITS, :], in_=gate_s.rearrange("(a w) -> a w", a=UNITS))
        nc.scalar.dma_start(
            out=sc_raw[UNITS : 2 * UNITS, :], in_=up_s.rearrange("(a w) -> a w", a=UNITS)
        )
        nc.scalar.activation(out=warm_out[:], in_=warm[:], func=SILU)

        x_sb = []
        for tt in range(TOK // P):
            x_tile = const.tile([P, H], BF16, name="x%d" % tt)
            nc.sync.dma_start(out=x_tile[:], in_=xf[P * tt : P * (tt + 1), :])
            x_sb.append(x_tile)

        gate_tiles = {}
        up_tiles = {}

        def load_unit(a):
            gate_tile = wpool.tile([P, 2 * H], BF16, name="gw%d" % a, tag="gw")
            nc.sync.dma_start(out=gate_tile[:], in_=gate_rows[a])
            up_tile = wpool.tile([P, 2 * H], BF16, name="uw%d" % a, tag="uw")
            nc.sync.dma_start(out=up_tile[:], in_=up_rows[a])
            gate_tiles[a] = gate_tile
            up_tiles[a] = up_tile

        for a in range(UNITS_IN_SBUF):
            load_unit(a)

        slabs = []
        down_s_all = const.tile([P, H], BF16, name="ds_bc")

        def load_down():
            for b in range(SLABS):
                slab = dpool.tile([P, INNER], BF16, name="dw%d" % b, tag="dw")
                nc.sync.dma_start(out=slab[:], in_=down_rows[b])
                slabs.append(slab)
            nc.sync.dma_start(out=down_s_all[:], in_=down_s.partition_broadcast(P))

        x_words = const.tile([P, 2 * TOK], U32, name="xc", align_bytes=64)
        x_plane = const.tile([P, 2 * TOK], U8, name="xs", align_bytes=64)
        hdn_words = const.tile([P, PASSES_2 * TOK], U32, name="hc", align_bytes=64)
        hdn_plane = const.tile([P, PASSES_2 * TOK], U8, name="hs", align_bytes=64)
        scale_pairs = const.tile([P, 2 * UNITS], F32, name="sc_w")
        scales_f32 = const.tile([P, 4 * UNITS], F32, name="sc_f")

        staging_of = {}
        codes_of = {}

        def transpose_unit(a):
            filled = []
            sources = ((gate_tiles[a], 0), (up_tiles[a], 0), (gate_tiles[a], 1), (up_tiles[a], 1))
            for j, (w_tile, e) in enumerate(sources):
                pairs = w_tile[:].bitcast(F32)
                squares = [pairs[:, BANK * e + P * n : BANK * e + P * (n + 1)] for n in range(4)]
                filled.append(transpose_into_bank("t%d_%d" % (a, j), squares))
            if a + UNITS_IN_SBUF < UNITS:
                load_unit(a + UNITS_IN_SBUF)
                if a + UNITS_IN_SBUF == UNITS - 1:
                    load_down()
            staging = spool.tile([P, STAGING], BF16, name="stg%d" % a, tag="stg", align_bytes=64)
            staging_of[a] = staging
            return filled

        def new_codes(a):
            words = cpool.tile([P, 1024], U32, name="wc%d" % a, tag="wc", align_bytes=64)
            plane = cpool.tile([P, 1024], U8, name="ws%d" % a, tag="ws", align_bytes=64)
            codes_of[a] = (words, plane)

        def quantise_unit(a, e):
            words, plane = codes_of[a]
            quantise(staging_of[a], e, words, plane, 512 * e)

        def mx_unit(a):
            words, plane = codes_of[a]
            sums = []
            for j in range(4):
                bank = next_bank("m%d_%d" % (a, j))
                for k1 in range(2):
                    w0 = 256 * j + P * k1
                    nc.tensor.matmul_mx(
                        out=bank[:],
                        lhsT=words[:, w0 : w0 + P].bitcast(FP8X4),
                        lhsT_scale=plane[:, w0 : w0 + P],
                        rhs=x_words[:, TOK * k1 : TOK * (k1 + 1)].bitcast(FP8X4),
                        rhs_scale=x_plane[:, TOK * k1 : TOK * (k1 + 1)],
                        start=(k1 == 0),
                        stop=(k1 == 1),
                    )
                sums.append(bank)
            return sums

        silu_of = {}
        four_planes_of = {}
        grouped_of = {}

        def silu(a, e, sums):
            silu_tile = epool.tile([P, TOK], F32, name="sl%d_%d" % (a, e), tag="sl", bufs=4)
            col = 2 * a + e
            nc.scalar.activation(
                out=silu_tile[:], in_=sums[2 * e][:], func=SILU, scale=scales_f32[:, col : col + 1]
            )
            silu_of[(a, e)] = silu_tile

        def product(a, e, sums):
            if a % 2 == 0 and e == 0:
                four = epool.tile([P, 4 * TOK], BF16, name="hsb%d" % (a // 2), tag="hsb")
                four_planes_of[a // 2] = four
            t = 2 * (a % 2) + e
            col = 2 * UNITS + 2 * a + e
            nc.vector.scalar_tensor_tensor(
                out=four_planes_of[a // 2][:, TOK * t : TOK * (t + 1)],
                in0=sums[2 * e + 1][:],
                scalar=scales_f32[:, col : col + 1],
                in1=silu_of[(a, e)][:],
                op0=MULT,
                op1=MULT,
            )

        def regroup(k2):
            grouped = epool.tile([P, 4 * TOK], BF16, name="hg%d" % k2, tag="hg", align_bytes=64)
            grouped_of[k2] = grouped
            nc.vector.tensor_copy(
                out=grouped[:].rearrange("p (c i t) -> p c t i", c=P, i=4, t=4),
                in_=four_planes_of[k2][:].rearrange("p (t c i) -> p c t i", t=4, c=P, i=4),
            )

        def quantise_hdn(k2):
            nc.vector.quantize_mx(
                out=hdn_words[:, TOK * k2 : TOK * (k2 + 1)].bitcast(FP8X4),
                scales=hdn_plane[:, TOK * k2 : TOK * (k2 + 1)],
                in_=grouped_of[k2][:],
            )

        down_staging_of = {}
        down_codes_of = {}

        def transpose_down(q, k2):
            squares = []
            for b in range(2):
                pairs = slabs[2 * q + b][:].bitcast(F32)
                for s in range(2):
                    first = 256 * k2 + P * s
                    squares.append(pairs[:, first : first + P])
            return transpose_into_bank("d%d_%d" % (q, k2), squares)

        def copy_down_out(engine, q, k2, bank):
            if k2 % 4 == 0:
                staging = spool.tile(
                    [P, STAGING], BF16, name="dstg%d_%d" % (q, k2 // 4), tag="stg", align_bytes=64
                )
                down_staging_of[(q, k2 // 4)] = staging
            copy_pairs_out(engine, room_for_bank(down_staging_of[(q, k2 // 4)], k2 % 4), bank)

        def quantise_down(q, n):
            if n == 0:
                words = dcpool.tile([P, PASSES_2 * 256], U32, name="dc%d" % q, tag="dc", align_bytes=64)
                plane = dcpool.tile([P, PASSES_2 * 256], U8, name="dsc%d" % q, tag="dsc", align_bytes=64)
                down_codes_of[q] = (words, plane)
            words, plane = down_codes_of[q]
            quantise(down_staging_of[(q, n // 2)], n % 2, words, plane, 512 * n)

        def mx2_pass(q, tt, k2, dst):
            words, plane = down_codes_of[q]
            w0 = TOK * k2 + P * tt
            nc.tensor.matmul_mx(
                out=dst,
                lhsT=hdn_words[:, w0 : w0 + P].bitcast(FP8X4),
                lhsT_scale=hdn_plane[:, w0 : w0 + P],
                rhs=words[:, 256 * k2 : 256 * (k2 + 1)].bitcast(FP8X4),
                rhs_scale=plane[:, 256 * k2 : 256 * (k2 + 1)],
                start=(k2 == 0),
                stop=(k2 == PASSES_2 - 1),
            )

        def scale_and_store(q, tt, sums):
            out_tile = opool.tile([P, 256], F32, name="o%d_%d" % (q, tt), tag="o")
            nc.vector.tensor_tensor(
                out=out_tile[:], in0=sums, in1=down_s_all[:, 256 * q : 256 * (q + 1)], op=MULT
            )
            nc.sync.dma_start(
                out=of[P * tt : P * (tt + 1), 256 * q : 256 * (q + 1)], in_=out_tile[:]
            )

        x_staging = spool.tile([P, STAGING], BF16, name="xg", tag="stg", align_bytes=64)
        x_rooms = x_staging[:].bitcast(F32).rearrange("p (i m s) -> p i m s", i=2, m=TOK, s=2)
        for tt in range(TOK // P):
            pairs = x_sb[tt][:].bitcast(F32)
            bank = transpose_into_bank("tx%d" % tt, [pairs[:, P * n : P * (n + 1)] for n in range(4)])
            copy_pairs_out("v" if tt % 2 == 0 else "s", x_rooms[:, :, P * tt : P * (tt + 1), :], bank)

        bank = transpose_into_bank("tsc", [sc_raw[:].bitcast(F32)])
        nc.vector.tensor_copy(out=scale_pairs[:], in_=bank[:, 0 : 2 * UNITS])
        nc.vector.tensor_copy(out=scales_f32[:], in_=scale_pairs[:].bitcast(BF16))
        quantise(x_staging, 0, x_words, x_plane, 0)
        quantise(x_staging, 1, x_words, x_plane, 512)

        filled = transpose_unit(0)
        new_codes(0)
        copy_pairs_out("s", room_for_bank(staging_of[0], 0), filled[0])
        copy_pairs_out("s", room_for_bank(staging_of[0], 1), filled[1])
        quantise_unit(0, 0)
        copy_pairs_out("s", room_for_bank(staging_of[0], 2), filled[2])
        copy_pairs_out("v", room_for_bank(staging_of[0], 3), filled[3])
        quantise_unit(0, 1)

        def copy_and_quantise_unit(a, filled_banks, hdn_pass):
            new_codes(a)
            for j in range(4):
                copy_pairs_out("s", room_for_bank(staging_of[a], j), filled_banks[j])
                if j % 2 == 1:
                    quantise_unit(a, j // 2)
                    if j == 1 and hdn_pass >= 0:
                        quantise_hdn(hdn_pass)

        def finish_units(units, sums_of):
            for a in units:
                silu(a, 0, sums_of[a])
                silu(a, 1, sums_of[a])
            for a in units:
                product(a, 0, sums_of[a])
                product(a, 1, sums_of[a])

        filled = transpose_unit(1)
        copy_and_quantise_unit(1, filled, -1)
        finish_units((0,), {0: mx_unit(0)})

        for k in range(UNITS // 2 - 1):
            first = 2 * k + 2
            filled_first = transpose_unit(first)
            filled_second = transpose_unit(first + 1)
            copy_and_quantise_unit(first, filled_first, k - 1)
            copy_and_quantise_unit(first + 1, filled_second, -1)
            sums_of = {}
            sums_of[first - 1] = mx_unit(first - 1)
            sums_of[first] = mx_unit(first)
            finish_units((first - 1, first), sums_of)
            regroup(k)

        first_down_banks = ((0, 0), (0, 1), (0, 2), (0, 3), (0, 4), (0, 5), (1, 0), (1, 1))
        filled = [transpose_down(q, k2) for q, k2 in first_down_banks]
        for n, (q, k2) in enumerate(first_down_banks):
            copy_down_out("s", q, k2, filled[n])
            if n % 2 == 1:
                quantise_down(q, k2 // 2)
                if n == 1:
                    quantise_hdn(PASSES_2 - 2)
        finish_units((UNITS - 1,), {UNITS - 1: mx_unit(UNITS - 1)})
        regroup(PASSES_2 - 1)

        filled = [transpose_down(1, k2) for k2 in range(2, PASSES_2)]
        for k2 in range(2, PASSES_2):
            copy_down_out("s", 1, k2, filled[k2 - 2])
            if k2 == 3:
                quantise_down(1, 1)
                quantise_hdn(PASSES_2 - 1)
        quantise_down(1, 2)

        out_banks = [next_bank("o0_%d" % tt) for tt in range(4)]
        for k2 in range(PASSES_2):
            for tt in range(4):
                mx2_pass(0, tt, k2, out_banks[tt][:, 0:256])
        for tt in range(4):
            scale_and_store(0, tt, out_banks[tt][:, 0:256])

        for q in (2, 3):
            filled = [transpose_down(q, k2) for k2 in range(PASSES_2)]
            for k2 in range(PASSES_2):
                copy_down_out("s" if k2 % 2 == 0 else "v", q, k2, filled[k2])
                if k2 == 3:
                    quantise_down(q, 0)
            quantise_down(q, 1)
            quantise_down(q, 2)
            out_banks = []
            for n in range(2):
                out_bank = next_bank("o%d_%d" % (q - 1, n))
                out_banks.append(out_bank)
                for side in range(2):
                    for k2 in range(PASSES_2):
                        mx2_pass(q - 1, 2 * n + side, k2, out_bank[:, 256 * side : 256 * (side + 1)])
            for tt in range(4):
                scale_and_store(q - 1, tt, out_banks[tt // 2][:, 256 * (tt % 2) : 256 * (tt % 2 + 1)])

        for tt in range(4):
            out_bank = next_bank("o3_%d" % tt)
            for k2 in range(PASSES_2):
                mx2_pass(3, tt, k2, out_bank[:, 0:256])
            scale_and_store(3, tt, out_bank[:, 0:256])
